import numpy as np
import ml_dtypes


def mxq(x, axis, fmt="e4m3"):
    dtype, down = {"e4m3": (ml_dtypes.float8_e4m3fn, 7), "e5m2": (ml_dtypes.float8_e5m2, 14)}[fmt]
    v = np.moveaxis(np.asarray(x, np.float32).astype(ml_dtypes.bfloat16).astype(np.float64), axis, -1)
    blocks = v.reshape(v.shape[:-1] + (-1, 32))
    amax = np.abs(blocks).max(-1, keepdims=True)
    byte = np.maximum(np.where(amax > 0, np.frexp(amax)[1] - 1 + 127, 0) - down, 1)
    scale = np.exp2(byte - 127.0)
    codes = (blocks / scale).astype(np.float32).astype(dtype).astype(np.float64)
    return np.moveaxis((codes * scale).reshape(v.shape), -1, axis)


WIDE = False


def mx_kscale(k):
    if not WIDE:
        return np.ones(k)
    levels = np.array([10, -10, 5, -5, 0])
    a = np.random.permutation(np.resize(levels, k // 512 * 4)).reshape(k // 512, 4)
    idx = np.arange(k)
    return np.exp2(a[idx // 512, idx % 128 // 32])


BF16 = ml_dtypes.bfloat16


def bf(x):
    return np.asarray(x, np.float32).astype(BF16)


def f64(x):
    return np.asarray(x).astype(np.float64)


B, N, D, R, Q = 4, 1024, 1024, 16, 16


def setup_inputs():
    s = mx_kscale(D)
    return {"x": bf(np.random.standard_normal((B, N, D)) * s),
            "w0": bf(np.random.standard_normal((B, N, R))),
            "core1": bf(np.random.standard_normal((R, D, Q)) / np.sqrt(D * R) / s[None, :, None]),
            "core2": bf(np.random.standard_normal((Q, D, R)) / np.sqrt(D * Q) / s[None, :, None])}


def reference(x, w0, core1, core2):
    xq = mxq(f64(x), 2, "e4m3")
    c1 = mxq(f64(core1), 1, "e4m3").transpose(1, 0, 2).reshape(D, R * Q)
    c2 = mxq(f64(core2), 1, "e4m3").transpose(1, 0, 2).reshape(D, Q * R)
    m1 = (xq @ c1).reshape(B, N, R, Q)
    m2 = (xq @ c2).reshape(B, N, Q, R)
    w1 = (f64(w0)[..., :, None] * m1).sum(-2)
    w2 = (w1[..., :, None] * m2).sum(-2)
    return w2

@@ -1,0 +1,141 @@
+from contextlib import ExitStack
+
+import concourse.mybir as mybir
+from concourse.masks import make_identity
+
+F32 = mybir.dt.float32
+BF16 = mybir.dt.bfloat16
+U32 = mybir.dt.uint32
+U8 = mybir.dt.uint8
+FP8X4 = mybir.dt.float8_e4m3fn_x4
+ADD = mybir.AluOpType.add
+MULT = mybir.AluOpType.mult
+AXIS_X = mybir.AxisListType.X
+
+P = 128
+TOKENS = 4096
+D = 1024
+R = 16
+TILES = TOKENS // P
+CH = 4
+NCH = TILES // CH
+FLOPS = 2 * TOKENS * D * 512 + 4 * TOKENS * 256
+
+
+def tile_linear_pa_kernel(tc, x, w0, core1, core2, out):
+    nc = tc.nc
+    xv = x.flatten_outer_dims().rearrange("(p j) d -> p j d", j=TILES)
+    w0v = w0.flatten_outer_dims().rearrange("(p j) r -> p (j r)", j=TILES)
+    outv = out.flatten_outer_dims().rearrange("(p j) r -> p j r", j=TILES)
+
+    with ExitStack() as ctx:
+        keep = ctx.enter_context(tc.tile_pool(name="keep", bufs=1))
+        stage = ctx.enter_context(tc.tile_pool(name="stage", bufs=3))
+        ps_t = ctx.enter_context(tc.psum_pool(name="ps_t", bufs=4))
+        ps_m = ctx.enter_context(tc.psum_pool(name="ps_m", bufs=4))
+
+        wraw = keep.tile([P, 4096], BF16)
+        xs = []
+        for c in range(NCH):
+            x_sb = keep.tile([P, CH, D], BF16, name="x_sb%d" % c)
+            xs.append(x_sb)
+        nc.sync.dma_start(out=xs[0][:], in_=xv[:, 0:CH, :])
+        for core, src in enumerate((core1, core2)):
+            nc.scalar.dma_start(
+                out=wraw[:, core * 2048:(core + 1) * 2048].rearrange("p (m f) -> p m f", f=32),
+                in_=src.rearrange("a (m p e) b -> p (a m) (e b)", m=4, p=P, e=2),
+            )
+        w0_sb = keep.tile([P, TILES * R], BF16)
+        nc.sync.dma_start(out=w0_sb[:], in_=w0v)
+        for c in range(1, NCH):
+            nc.sync.dma_start(out=xs[c][:], in_=xv[:, c * CH:(c + 1) * CH, :])
+
+        ident = keep.tile([P, P], F32)
+        make_identity(nc, ident[:])
+
+        out_sb = keep.tile([P, TILES * R], F32)
+
+        wgrp = keep.tile([P, 2, 2048], BF16, align_bytes=64)
+        wcodes = keep.tile([P, 2, 512], U32, align_bytes=64)
+        wscales = keep.tile([P, 2, 512], U8, align_bytes=64)
+        wview = wraw[:].rearrange("p (c a g u e b) -> p c a g u e b", c=2, a=16, g=2, u=2, e=2)
+
+        def weights():
+            for core in range(2):
+                for g in range(2):
+                    nc.vector.tensor_copy(
+                        out=wgrp[:, g, core * 1024:(core + 1) * 1024].rearrange(
+                            "p (b a u e) -> p b a u e", b=16, a=16, u=2),
+                        in_=wview[:, core, :, g].rearrange("p a u e b -> p b a u e"),
+                    )
+            for g in range(2):
+                nc.vector.quantize_mx(
+                    out=wcodes[:, g, :].bitcast(FP8X4), scales=wscales[:, g, :], in_=wgrp[:, g, :])
+
+        xq = {}
+
+        def front(c):
+            grouped = stage.tile([P, CH * 1024], BF16, align_bytes=64, tag="grouped")
+            for jj in range(CH):
+                xt = ps_t.tile([P, 512], F32, tag="xt")
+                xw = xs[c][:, jj, :].bitcast(F32)
+                for k in range(4):
+                    nc.tensor.transpose(xt[:, k * P:(k + 1) * P], xw[:, k * P:(k + 1) * P], ident[:])
+                nc.scalar.copy(
+                    out=grouped[:, jj * 1024:(jj + 1) * 1024].bitcast(F32).rearrange(
+                        "p (g r u) -> p g r u", g=2, u=2),
+                    in_=xt[:].rearrange("p (g u r) -> p g r u", g=2, u=2),
+                )
+            codes = stage.tile([P, CH * 256], U32, align_bytes=64, tag="codes")
+            scales = stage.tile([P, CH * 256], U8, align_bytes=64, tag="scales")
+            nc.vector.quantize_mx(out=codes[:].bitcast(FP8X4), scales=scales[:], in_=grouped[:])
+            xq[c] = (codes, scales)
+
+        def back(c):
+            codes, scales = xq[c]
+            p1 = stage.tile([P, CH, 256], F32, tag="p1")
+            p2 = stage.tile([P, CH, 256], F32, tag="p2")
+            w1 = stage.tile([P, CH * 16], F32, tag="w1")
+            mms = []
+            for jj in range(CH):
+                mm = ps_m.tile([P, 512], F32, tag="mm")
+                mms.append(mm)
+                for g in range(2):
+                    cols = slice((jj * 2 + g) * P, (jj * 2 + g + 1) * P)
+                    nc.tensor.matmul_mx(
+                        out=mm[:],
+                        lhsT=codes[:, cols].bitcast(FP8X4), lhsT_scale=scales[:, cols],
+                        rhs=wcodes[:, g, :].bitcast(FP8X4), rhs_scale=wscales[:, g, :],
+                        start=(g == 0), stop=(g == 1),
+                    )
+                j = c * CH + jj
+                nc.vector.tensor_tensor(
+                    out=p1[:, jj, :].rearrange("p (q r) -> p q r", r=16),
+                    in0=mm[:, 0:256].rearrange("p (q r) -> p q r", r=16),
+                    in1=w0_sb[:, j * R:(j + 1) * R].unsqueeze(1).to_broadcast([P, 16, 16]),
+                    op=MULT,
+                )
+            nc.vector.tensor_reduce(
+                out=w1[:], in_=p1[:].rearrange("p c (q r) -> p (c q) r", r=16), axis=AXIS_X, op=ADD)
+            for jj in range(CH):
+                nc.vector.tensor_tensor(
+                    out=p2[:, jj, :].rearrange("p (r q) -> p r q", q=16),
+                    in0=mms[jj][:, 256:512].rearrange("p (r q) -> p r q", q=16),
+                    in1=w1[:, jj * 16:(jj + 1) * 16].unsqueeze(1).to_broadcast([P, 16, 16]),
+                    op=MULT,
+                )
+            o_cols = slice(c * CH * R, (c + 1) * CH * R)
+            nc.vector.tensor_reduce(
+                out=out_sb[:, o_cols], in_=p2[:].rearrange("p c (r q) -> p (c r) q", q=16),
+                axis=AXIS_X, op=ADD)
+            nc.sync.dma_start(
+                out=outv[:, c * CH:(c + 1) * CH, :],
+                in_=out_sb[:, o_cols].rearrange("p (c r) -> p c r", r=R))
+
+        front(0)
+        weights()
+        front(1)
+        for c in range(NCH):
+            if c + 2 < NCH:
+                front(c + 2)
+            back(c)

@@ -30,15 +30,23 @@ def tile_linear_pa_kernel(tc, x, w0, core1, core2, out):
 
     with ExitStack() as ctx:
         keep = ctx.enter_context(tc.tile_pool(name="keep", bufs=1))
-        stage = ctx.enter_context(tc.tile_pool(name="stage", bufs=3))
+        stage = ctx.enter_context(tc.tile_pool(name="stage", bufs=2))
         ps_t = ctx.enter_context(tc.psum_pool(name="ps_t", bufs=4))
-        ps_m = ctx.enter_context(tc.psum_pool(name="ps_m", bufs=4))
+        ps_a = ctx.enter_context(tc.psum_pool(name="ps_a", bufs=2))
+        ps_b = ctx.enter_context(tc.psum_pool(name="ps_b", bufs=2))
+        ctx.enter_context(tc.manual_schedule())
 
         wraw = keep.tile([P, 4096], BF16)
         xs = []
+        xcodes = []
+        xscales = []
         for c in range(NCH):
             x_sb = keep.tile([P, CH, D], BF16, name="x_sb%d" % c)
             xs.append(x_sb)
+            codes = keep.tile([P, CH * 256], U32, align_bytes=64, name="codes%d" % c)
+            xcodes.append(codes)
+            scales = keep.tile([P, CH * 256], U8, align_bytes=64, name="scales%d" % c)
+            xscales.append(scales)
         nc.sync.dma_start(out=xs[0][:], in_=xv[:, 0:CH, :])
         for core, src in enumerate((core1, core2)):
             nc.scalar.dma_start(
@@ -52,7 +60,6 @@ def tile_linear_pa_kernel(tc, x, w0, core1, core2, out):
 
         ident = keep.tile([P, P], F32)
         make_identity(nc, ident[:])
-
         out_sb = keep.tile([P, TILES * R], F32)
 
         wgrp = keep.tile([P, 2, 2048], BF16, align_bytes=64)
@@ -61,21 +68,29 @@ def tile_linear_pa_kernel(tc, x, w0, core1, core2, out):
         wview = wraw[:].rearrange("p (c a g u e b) -> p c a g u e b", c=2, a=16, g=2, u=2, e=2)
 
         def weights():
-            for core in range(2):
-                for g in range(2):
-                    nc.vector.tensor_copy(
-                        out=wgrp[:, g, core * 1024:(core + 1) * 1024].rearrange(
-                            "p (b a u e) -> p b a u e", b=16, a=16, u=2),
-                        in_=wview[:, core, :, g].rearrange("p a u e b -> p b a u e"),
-                    )
+            for g in range(2):
+                nc.vector.tensor_copy(
+                    out=wgrp[:, g, 0:1024].rearrange("p (b a u e) -> p b a u e", b=16, a=16, u=2),
+                    in_=wview[:, 0, :, g].rearrange("p a u e b -> p b a u e"),
+                )
+            for g in range(2):
+                nc.vector.tensor_copy(
+                    out=wgrp[:, g, 1024:2048].rearrange("p (a b u e) -> p a b u e", b=16, a=16, u=2),
+                    in_=wview[:, 1, :, g].rearrange("p a u e b -> p a b u e"),
+                )
             for g in range(2):
                 nc.vector.quantize_mx(
                     out=wcodes[:, g, :].bitcast(FP8X4), scales=wscales[:, g, :], in_=wgrp[:, g, :])
 
-        xq = {}
+        grouped_of = {}
+        bank_of = {}
+        p1_of = {}
+        p2_of = {}
+        w1_of = {}
 
-        def front(c):
+        def transposes(c):
             grouped = stage.tile([P, CH * 1024], BF16, align_bytes=64, tag="grouped")
+            grouped_of[c] = grouped
             for jj in range(CH):
                 xt = ps_t.tile([P, 512], F32, tag="xt")
                 xw = xs[c][:, jj, :].bitcast(F32)
@@ -86,56 +101,90 @@ def tile_linear_pa_kernel(tc, x, w0, core1, core2, out):
                         "p (g r u) -> p g r u", g=2, u=2),
                     in_=xt[:].rearrange("p (g u r) -> p g r u", g=2, u=2),
                 )
-            codes = stage.tile([P, CH * 256], U32, align_bytes=64, tag="codes")
-            scales = stage.tile([P, CH * 256], U8, align_bytes=64, tag="scales")
-            nc.vector.quantize_mx(out=codes[:].bitcast(FP8X4), scales=scales[:], in_=grouped[:])
-            xq[c] = (codes, scales)
 
-        def back(c):
-            codes, scales = xq[c]
-            p1 = stage.tile([P, CH, 256], F32, tag="p1")
-            p2 = stage.tile([P, CH, 256], F32, tag="p2")
+        def quantise(c):
+            nc.vector.quantize_mx(
+                out=xcodes[c][:].bitcast(FP8X4), scales=xscales[c][:], in_=grouped_of[c][:])
+
+        def passes(c, core):
+            pool = ps_a if core == 0 else ps_b
+            for h in range(2):
+                bank = pool.tile([P, 512], F32, tag="bank%d" % core)
+                bank_of[(c, core, h)] = bank
+                for t in range(2):
+                    jj = 2 * h + t
+                    for g in range(2):
+                        cols = slice((jj * 2 + g) * P, (jj * 2 + g + 1) * P)
+                        nc.tensor.matmul_mx(
+                            out=bank[:, t * 256:(t + 1) * 256],
+                            lhsT=xcodes[c][:, cols].bitcast(FP8X4), lhsT_scale=xscales[c][:, cols],
+                            rhs=wcodes[:, g, core * 256:(core + 1) * 256].bitcast(FP8X4),
+                            rhs_scale=wscales[:, g, core * 256:(core + 1) * 256],
+                            start=(g == 0), stop=(g == 1),
+                        )
+
+        def mult_a(c):
+            p1 = stage.tile([P, CH * 256], F32, tag="p1")
+            p1_of[c] = p1
+            for h in range(2):
+                j0 = c * CH + 2 * h
+                nc.vector.tensor_tensor(
+                    out=p1[:, h * 512:(h + 1) * 512].rearrange("p (t q r) -> p t q r", t=2, q=16),
+                    in0=bank_of[(c, 0, h)][:].rearrange("p (t q r) -> p t q r", t=2, q=16),
+                    in1=w0_sb[:, j0 * R:(j0 + 2) * R].rearrange(
+                        "p (t r) -> p t r", t=2).unsqueeze(2).to_broadcast([P, 2, 16, 16]),
+                    op=MULT,
+                )
+
+        def sum_a(c):
             w1 = stage.tile([P, CH * 16], F32, tag="w1")
-            mms = []
-            for jj in range(CH):
-                mm = ps_m.tile([P, 512], F32, tag="mm")
-                mms.append(mm)
-                for g in range(2):
-                    cols = slice((jj * 2 + g) * P, (jj * 2 + g + 1) * P)
-                    nc.tensor.matmul_mx(
-                        out=mm[:],
-                        lhsT=codes[:, cols].bitcast(FP8X4), lhsT_scale=scales[:, cols],
-                        rhs=wcodes[:, g, :].bitcast(FP8X4), rhs_scale=wscales[:, g, :],
-                        start=(g == 0), stop=(g == 1),
-                    )
-                j = c * CH + jj
-                nc.vector.tensor_tensor(
-                    out=p1[:, jj, :].rearrange("p (q r) -> p q r", r=16),
-                    in0=mm[:, 0:256].rearrange("p (q r) -> p q r", r=16),
-                    in1=w0_sb[:, j * R:(j + 1) * R].unsqueeze(1).to_broadcast([P, 16, 16]),
-                    op=MULT,
-                )
+            w1_of[c] = w1
             nc.vector.tensor_reduce(
-                out=w1[:], in_=p1[:].rearrange("p c (q r) -> p (c q) r", r=16), axis=AXIS_X, op=ADD)
-            for jj in range(CH):
-                nc.vector.tensor_tensor(
-                    out=p2[:, jj, :].rearrange("p (r q) -> p r q", q=16),
-                    in0=mms[jj][:, 256:512].rearrange("p (r q) -> p r q", q=16),
-                    in1=w1[:, jj * 16:(jj + 1) * 16].unsqueeze(1).to_broadcast([P, 16, 16]),
-                    op=MULT,
-                )
-            o_cols = slice(c * CH * R, (c + 1) * CH * R)
-            nc.vector.tensor_reduce(
-                out=out_sb[:, o_cols], in_=p2[:].rearrange("p c (r q) -> p (c r) q", q=16),
-                axis=AXIS_X, op=ADD)
-            nc.sync.dma_start(
-                out=outv[:, c * CH:(c + 1) * CH, :],
-                in_=out_sb[:, o_cols].rearrange("p (c r) -> p c r", r=R))
+                out=w1[:], in_=p1_of[c][:].rearrange("p (n r) -> p n r", r=16), axis=AXIS_X, op=ADD)
 
-        front(0)
-        weights()
-        front(1)
-        for c in range(NCH):
-            if c + 2 < NCH:
-                front(c + 2)
-            back(c)
+        def mult_b(c):
+            p2 = stage.tile([P, CH, 256], F32, tag="p2")
+            p2_of[c] = p2
+            for h in range(2):
+                nc.vector.tensor_tensor(
+                    out=p2[:, 2 * h:2 * h + 2, :].rearrange("p t (q r) -> p t q r", q=16),
+                    in0=bank_of[(c, 1, h)][:].rearrange("p (t q r) -> p t q r", t=2, q=16),
+                    in1=w1_of[c][:, h * 32:(h + 1) * 32].rearrange(
+                        "p (t q) -> p t q", t=2).unsqueeze(3).to_broadcast([P, 2, 16, 16]),
+                    op=MULT,
+                )
+
+        def sum_b(c):
+            p2 = p2_of[c]
+            o_view = out_sb[:, c * CH * R:(c + 1) * CH * R].rearrange("p (t r) -> p t r", r=R)
+            if c == NCH - 1:
+                nc.vector.tensor_reduce(
+                    out=o_view, in_=p2[:].rearrange("p t (q r) -> p t r q", q=16), axis=AXIS_X, op=ADD)
+            else:
+                for half in (128, 64, 32):
+                    nc.gpsimd.tensor_tensor(
+                        out=p2[:, :, 0:half], in0=p2[:, :, 0:half], in1=p2[:, :, half:2 * half], op=ADD)
+                nc.gpsimd.tensor_tensor(out=o_view, in0=p2[:, :, 0:16], in1=p2[:, :, 16:32], op=ADD)
+            nc.sync.dma_start(out=outv[:, c * CH:(c + 1) * CH, :], in_=o_view)
+
+        def live(c):
+            return 0 <= c < NCH
+
+        for i in range(-4, NCH):
+            if live(i + 4):
+                transposes(i + 4)
+            if live(i + 3):
+                quantise(i + 3)
+            if i == -2:
+                weights()
+            if live(i):
+                mult_b(i)
+            if live(i + 1):
+                passes(i + 1, 1)
+                mult_a(i + 1)
+            if live(i + 2):
+                passes(i + 2, 0)
+            if live(i + 1):
+                sum_a(i + 1)
+            if live(i):
+                sum_b(i)

@@ -36,7 +36,7 @@ def tile_linear_pa_kernel(tc, x, w0, core1, core2, out):
         ps_b = ctx.enter_context(tc.psum_pool(name="ps_b", bufs=2))
         ctx.enter_context(tc.manual_schedule())
 
-        wraw = keep.tile([P, 4096], BF16)
+        wl = keep.tile([P, 4096], BF16)
         xs = []
         xcodes = []
         xscales = []
@@ -47,15 +47,11 @@ def tile_linear_pa_kernel(tc, x, w0, core1, core2, out):
             xcodes.append(codes)
             scales = keep.tile([P, CH * 256], U8, align_bytes=64, name="scales%d" % c)
             xscales.append(scales)
-        nc.sync.dma_start(out=xs[0][:], in_=xv[:, 0:CH, :])
-        for core, src in enumerate((core1, core2)):
-            nc.scalar.dma_start(
-                out=wraw[:, core * 2048:(core + 1) * 2048].rearrange("p (m f) -> p m f", f=32),
-                in_=src.rearrange("a (m p e) b -> p (a m) (e b)", m=4, p=P, e=2),
-            )
+        nc.sync.dma_start(out=wl[0:64, :], in_=core1.rearrange("a (c l) b -> (a c) (l b)", c=4))
+        nc.scalar.dma_start(out=wl[64:128, :], in_=core2.rearrange("a (c l) b -> (a c) (l b)", c=4))
         w0_sb = keep.tile([P, TILES * R], BF16)
-        nc.sync.dma_start(out=w0_sb[:], in_=w0v)
-        for c in range(1, NCH):
+        nc.scalar.dma_start(out=w0_sb[:], in_=w0v)
+        for c in range(NCH):
             nc.sync.dma_start(out=xs[c][:], in_=xv[:, c * CH:(c + 1) * CH, :])
 
         ident = keep.tile([P, P], F32)
@@ -65,19 +61,38 @@ def tile_linear_pa_kernel(tc, x, w0, core1, core2, out):
         wgrp = keep.tile([P, 2, 2048], BF16, align_bytes=64)
         wcodes = keep.tile([P, 2, 512], U32, align_bytes=64)
         wscales = keep.tile([P, 2, 512], U8, align_bytes=64)
-        wview = wraw[:].rearrange("p (c a g u e b) -> p c a g u e b", c=2, a=16, g=2, u=2, e=2)
+        wd = keep.tile([P, 4096], BF16)
 
         def weights():
+            wl_v = wl[:].rearrange("p (l b) -> p l b", b=16)
+            for k, eng in ((0, "v"), (2, "s"), (3, "g"), (1, "v")):
+                dst = wd[:, k * 1024:(k + 1) * 1024].rearrange("p (b l) -> p l b", b=4)
+                src = wl_v[:, :, 4 * k:4 * k + 4]
+                if eng == "v":
+                    nc.vector.tensor_copy(out=dst, in_=src)
+                elif eng == "s":
+                    nc.scalar.copy(out=dst, in_=src)
+                else:
+                    nc.gpsimd.tensor_scalar(out=dst, in0=src, scalar1=1.0, scalar2=0.0, op0=MULT, op1=ADD)
+            wts = []
+            for k in range(4):
+                pool = ps_a if k < 2 else ps_b
+                wt = pool.tile([P, 512], F32, tag="bank%d" % (k // 2))
+                wts.append(wt)
+                for bb in range(4):
+                    b = 4 * k + bb
+                    nc.tensor.transpose(
+                        wt[:, bb * P:(bb + 1) * P], wd[:, b * 256:(b + 1) * 256].bitcast(F32), ident[:])
             for g in range(2):
-                nc.vector.tensor_copy(
-                    out=wgrp[:, g, 0:1024].rearrange("p (b a u e) -> p b a u e", b=16, a=16, u=2),
-                    in_=wview[:, 0, :, g].rearrange("p a u e b -> p b a u e"),
-                )
-            for g in range(2):
-                nc.vector.tensor_copy(
-                    out=wgrp[:, g, 1024:2048].rearrange("p (a b u e) -> p a b u e", b=16, a=16, u=2),
-                    in_=wview[:, 1, :, g].rearrange("p a u e b -> p a b u e"),
-                )
+                for k in range(4):
+                    dst = wgrp[:, g, :].bitcast(F32).rearrange(
+                        "p (c b a u) -> p b c a u", c=2, b=16, a=16)[:, 4 * k:4 * k + 4]
+                    src = wts[k][:].rearrange(
+                        "p (b c a g u) -> p g b c a u", b=4, c=2, a=16, g=2)[:, g]
+                    if k < 2:
+                        nc.vector.tensor_copy(out=dst, in_=src)
+                    else:
+                        nc.scalar.copy(out=dst, in_=src)
             for g in range(2):
                 nc.vector.quantize_mx(
                     out=wcodes[:, g, :].bitcast(FP8X4), scales=wscales[:, g, :], in_=wgrp[:, g, :])
@@ -88,23 +103,31 @@ def tile_linear_pa_kernel(tc, x, w0, core1, core2, out):
         p2_of = {}
         w1_of = {}
 
-        def transposes(c):
-            grouped = stage.tile([P, CH * 1024], BF16, align_bytes=64, tag="grouped")
-            grouped_of[c] = grouped
-            for jj in range(CH):
+        def transposes(c, tiles, on_vector=()):
+            if c not in grouped_of:
+                new_grouped = stage.tile([P, CH * 1024], BF16, align_bytes=64, tag="grouped")
+                grouped_of[c] = new_grouped
+            grouped = grouped_of[c]
+            for jj in tiles:
                 xt = ps_t.tile([P, 512], F32, tag="xt")
                 xw = xs[c][:, jj, :].bitcast(F32)
                 for k in range(4):
                     nc.tensor.transpose(xt[:, k * P:(k + 1) * P], xw[:, k * P:(k + 1) * P], ident[:])
-                nc.scalar.copy(
-                    out=grouped[:, jj * 1024:(jj + 1) * 1024].bitcast(F32).rearrange(
-                        "p (g r u) -> p g r u", g=2, u=2),
-                    in_=xt[:].rearrange("p (g u r) -> p g r u", g=2, u=2),
-                )
+                dst = grouped[:, jj * 1024:(jj + 1) * 1024].bitcast(F32).rearrange(
+                    "p (g r u) -> p g r u", g=2, u=2)
+                src = xt[:].rearrange("p (g u r) -> p g r u", g=2, u=2)
+                if jj in on_vector:
+                    nc.vector.tensor_copy(out=dst, in_=src)
+                else:
+                    nc.scalar.copy(out=dst, in_=src)
 
-        def quantise(c):
-            nc.vector.quantize_mx(
-                out=xcodes[c][:].bitcast(FP8X4), scales=xscales[c][:], in_=grouped_of[c][:])
+        def quantise(c, parts=1):
+            w = CH * 256 // parts
+            for h in range(parts):
+                nc.vector.quantize_mx(
+                    out=xcodes[c][:, h * w:(h + 1) * w].bitcast(FP8X4),
+                    scales=xscales[c][:, h * w:(h + 1) * w],
+                    in_=grouped_of[c][:, 4 * h * w:4 * (h + 1) * w])
 
         def passes(c, core):
             pool = ps_a if core == 0 else ps_b
@@ -148,7 +171,7 @@ def tile_linear_pa_kernel(tc, x, w0, core1, core2, out):
             for h in range(2):
                 nc.vector.tensor_tensor(
                     out=p2[:, 2 * h:2 * h + 2, :].rearrange("p t (q r) -> p t q r", q=16),
-                    in0=bank_of[(c, 1, h)][:].rearrange("p (t q r) -> p t q r", t=2, q=16),
+                    in0=bank_of[(c, 1, h)][:].rearrange("p (t r q) -> p t q r", t=2, q=16),
                     in1=w1_of[c][:, h * 32:(h + 1) * 32].rearrange(
                         "p (t q) -> p t q", t=2).unsqueeze(3).to_broadcast([P, 2, 16, 16]),
                     op=MULT,
@@ -170,21 +193,24 @@ def tile_linear_pa_kernel(tc, x, w0, core1, core2, out):
         def live(c):
             return 0 <= c < NCH
 
-        for i in range(-4, NCH):
-            if live(i + 4):
-                transposes(i + 4)
-            if live(i + 3):
-                quantise(i + 3)
-            if i == -2:
-                weights()
-            if live(i):
-                mult_b(i)
-            if live(i + 1):
-                passes(i + 1, 1)
-                mult_a(i + 1)
-            if live(i + 2):
-                passes(i + 2, 0)
-            if live(i + 1):
-                sum_a(i + 1)
-            if live(i):
-                sum_b(i)
+        whole = (0, 1, 2, 3)
+        weights()
+        transposes(0, whole, on_vector=(3,))
+        quantise(0, parts=2)
+        transposes(1, (0, 1))
+        passes(0, 0)
+        transposes(1, (2, 3))
+        passes(0, 1)
+        transposes(2, whole)
+        for c in range(NCH):
+            mult_a(c)
+            sum_a(c)
+            if live(c + 1):
+                quantise(c + 1)
+                passes(c + 1, 0)
+            mult_b(c)
+            if live(c + 1):
+                passes(c + 1, 1)
+            if live(c + 3):
+                transposes(c + 3, whole)
+            sum_b(c)

@@ -30,7 +30,7 @@ def tile_linear_pa_kernel(tc, x, w0, core1, core2, out):
 
     with ExitStack() as ctx:
         keep = ctx.enter_context(tc.tile_pool(name="keep", bufs=1))
-        stage = ctx.enter_context(tc.tile_pool(name="stage", bufs=2))
+        stage = ctx.enter_context(tc.tile_pool(name="stage", bufs=3))
         ps_t = ctx.enter_context(tc.psum_pool(name="ps_t", bufs=4))
         ps_a = ctx.enter_context(tc.psum_pool(name="ps_a", bufs=2))
         ps_b = ctx.enter_context(tc.psum_pool(name="ps_b", bufs=2))
@@ -83,16 +83,20 @@ def tile_linear_pa_kernel(tc, x, w0, core1, core2, out):
                     b = 4 * k + bb
                     nc.tensor.transpose(
                         wt[:, bb * P:(bb + 1) * P], wd[:, b * 256:(b + 1) * 256].bitcast(F32), ident[:])
+            words = wgrp[:].rearrange("p g n -> p (g n)").bitcast(F32)
+            dst1 = words.rearrange("p (g c b a u) -> p c g b a u", g=2, c=2, b=16, a=16)[:, 0]
+            dst2 = words.rearrange("p (g c a b u) -> p c g a b u", g=2, c=2, b=16, a=16)[:, 1]
+            for k in range(2):
+                src = wts[k][:].rearrange("p (b c a g u) -> p c g b a u", b=4, c=2, a=16, g=2)
+                nc.vector.tensor_copy(out=dst1[:, :, 4 * k:4 * k + 4], in_=src[:, 0])
+                nc.vector.tensor_copy(
+                    out=dst2[:, :, :, 4 * k:4 * k + 4], in_=src[:, 1].rearrange("p g b a u -> p g a b u"))
             for g in range(2):
-                for k in range(4):
-                    dst = wgrp[:, g, :].bitcast(F32).rearrange(
-                        "p (c b a u) -> p b c a u", c=2, b=16, a=16)[:, 4 * k:4 * k + 4]
-                    src = wts[k][:].rearrange(
-                        "p (b c a g u) -> p g b c a u", b=4, c=2, a=16, g=2)[:, g]
-                    if k < 2:
-                        nc.vector.tensor_copy(out=dst, in_=src)
-                    else:
-                        nc.scalar.copy(out=dst, in_=src)
+                for k in range(2, 4):
+                    src = wts[k][:].rearrange("p (b c a g u) -> p c g b a u", b=4, c=2, a=16, g=2)
+                    nc.scalar.copy(out=dst1[:, g, 4 * k:4 * k + 4], in_=src[:, 0, g])
+                    nc.scalar.copy(
+                        out=dst2[:, g, :, 4 * k:4 * k + 4], in_=src[:, 1, g].rearrange("p b a u -> p a b u"))
             for g in range(2):
                 nc.vector.quantize_mx(
                     out=wcodes[:, g, :].bitcast(FP8X4), scales=wscales[:, g, :], in_=wgrp[:, g, :])
@@ -171,7 +175,7 @@ def tile_linear_pa_kernel(tc, x, w0, core1, core2, out):
             for h in range(2):
                 nc.vector.tensor_tensor(
                     out=p2[:, 2 * h:2 * h + 2, :].rearrange("p t (q r) -> p t q r", q=16),
-                    in0=bank_of[(c, 1, h)][:].rearrange("p (t r q) -> p t q r", t=2, q=16),
+                    in0=bank_of[(c, 1, h)][:].rearrange("p (t q r) -> p t q r", t=2, q=16),
                     in1=w1_of[c][:, h * 32:(h + 1) * 32].rearrange(
                         "p (t q) -> p t q", t=2).unsqueeze(3).to_broadcast([P, 2, 16, 16]),
                     op=MULT,
@@ -180,14 +184,11 @@ def tile_linear_pa_kernel(tc, x, w0, core1, core2, out):
         def sum_b(c):
             p2 = p2_of[c]
             o_view = out_sb[:, c * CH * R:(c + 1) * CH * R].rearrange("p (t r) -> p t r", r=R)
-            if c == NCH - 1:
-                nc.vector.tensor_reduce(
-                    out=o_view, in_=p2[:].rearrange("p t (q r) -> p t r q", q=16), axis=AXIS_X, op=ADD)
-            else:
-                for half in (128, 64, 32):
-                    nc.gpsimd.tensor_tensor(
-                        out=p2[:, :, 0:half], in0=p2[:, :, 0:half], in1=p2[:, :, half:2 * half], op=ADD)
-                nc.gpsimd.tensor_tensor(out=o_view, in0=p2[:, :, 0:16], in1=p2[:, :, 16:32], op=ADD)
+            eng = nc.vector if c == NCH - 1 else nc.gpsimd
+            for half in (128, 64, 32):
+                eng.tensor_tensor(
+                    out=p2[:, :, 0:half], in0=p2[:, :, 0:half], in1=p2[:, :, half:2 * half], op=ADD)
+            eng.tensor_tensor(out=o_view, in0=p2[:, :, 0:16], in1=p2[:, :, 16:32], op=ADD)
             nc.sync.dma_start(out=outv[:, c * CH:(c + 1) * CH, :], in_=o_view)
 
         def live(c):
@@ -202,15 +203,25 @@ def tile_linear_pa_kernel(tc, x, w0, core1, core2, out):
         transposes(1, (2, 3))
         passes(0, 1)
         transposes(2, whole)
-        for c in range(NCH):
+        mult_a(0)
+        sum_a(0)
+        quantise(1)
+        passes(1, 0)
+        mult_b(0)
+        transposes(3, whole)
+        passes(1, 1)
+        sum_b(0)
+        quantise(2)
+        for c in range(1, NCH):
             mult_a(c)
-            sum_a(c)
             if live(c + 1):
-                quantise(c + 1)
                 passes(c + 1, 0)
+            sum_a(c)
+            if live(c + 2):
+                quantise(c + 2)
+            if live(c + 3):
+                transposes(c + 3, whole)
             mult_b(c)
             if live(c + 1):
                 passes(c + 1, 1)
-            if live(c + 3):
-                transposes(c + 3, whole)
             sum_b(c)

@@ -201,27 +201,22 @@ def tile_linear_pa_kernel(tc, x, w0, core1, core2, out):
         transposes(1, (0, 1))
         passes(0, 0)
         transposes(1, (2, 3))
-        passes(0, 1)
         transposes(2, whole)
         mult_a(0)
         sum_a(0)
         quantise(1)
         passes(1, 0)
-        mult_b(0)
-        transposes(3, whole)
-        passes(1, 1)
-        sum_b(0)
-        quantise(2)
-        for c in range(1, NCH):
-            mult_a(c)
-            if live(c + 1):
-                passes(c + 1, 0)
-            sum_a(c)
+        for c in range(NCH):
             if live(c + 2):
                 quantise(c + 2)
+            passes(c, 1)
+            if c > 0:
+                sum_a(c)
             if live(c + 3):
                 transposes(c + 3, whole)
-            mult_b(c)
             if live(c + 1):
-                passes(c + 1, 1)
+                mult_a(c + 1)
+            if live(c + 2):
+                passes(c + 2, 0)
+            mult_b(c)
             sum_b(c)

@@ -47,8 +47,8 @@ def tile_linear_pa_kernel(tc, x, w0, core1, core2, out):
             xcodes.append(codes)
             scales = keep.tile([P, CH * 256], U8, align_bytes=64, name="scales%d" % c)
             xscales.append(scales)
-        nc.sync.dma_start(out=wl[0:64, :], in_=core1.rearrange("a (c l) b -> (a c) (l b)", c=4))
-        nc.scalar.dma_start(out=wl[64:128, :], in_=core2.rearrange("a (c l) b -> (a c) (l b)", c=4))
+        nc.sync.dma_start(out=wl[0:128:2, :], in_=core1.rearrange("a (c l) b -> (a c) (l b)", c=4))
+        nc.scalar.dma_start(out=wl[1:128:2, :], in_=core2.rearrange("a (c l) b -> (a c) (l b)", c=4))
         w0_sb = keep.tile([P, TILES * R], BF16)
         nc.scalar.dma_start(out=w0_sb[:], in_=w0v)
         for c in range(NCH):
@@ -87,19 +87,31 @@ def tile_linear_pa_kernel(tc, x, w0, core1, core2, out):
             dst1 = words.rearrange("p (g c b a u) -> p c g b a u", g=2, c=2, b=16, a=16)[:, 0]
             dst2 = words.rearrange("p (g c a b u) -> p c g a b u", g=2, c=2, b=16, a=16)[:, 1]
             for k in range(2):
-                src = wts[k][:].rearrange("p (b c a g u) -> p c g b a u", b=4, c=2, a=16, g=2)
+                src = wts[k][:].rearrange("p (b a g u c) -> p c g b a u", b=4, c=2, a=16, g=2)
                 nc.vector.tensor_copy(out=dst1[:, :, 4 * k:4 * k + 4], in_=src[:, 0])
                 nc.vector.tensor_copy(
                     out=dst2[:, :, :, 4 * k:4 * k + 4], in_=src[:, 1].rearrange("p g b a u -> p g a b u"))
             for g in range(2):
                 for k in range(2, 4):
-                    src = wts[k][:].rearrange("p (b c a g u) -> p c g b a u", b=4, c=2, a=16, g=2)
+                    src = wts[k][:].rearrange("p (b a g u c) -> p c g b a u", b=4, c=2, a=16, g=2)
                     nc.scalar.copy(out=dst1[:, g, 4 * k:4 * k + 4], in_=src[:, 0, g])
-                    nc.scalar.copy(
-                        out=dst2[:, g, :, 4 * k:4 * k + 4], in_=src[:, 1, g].rearrange("p b a u -> p a b u"))
+            quantise_core(0)
+            return wts, dst2
+
+        def quantise_core(core):
             for g in range(2):
                 nc.vector.quantize_mx(
-                    out=wcodes[:, g, :].bitcast(FP8X4), scales=wscales[:, g, :], in_=wgrp[:, g, :])
+                    out=wcodes[:, g, core * 256:(core + 1) * 256].bitcast(FP8X4),
+                    scales=wscales[:, g, core * 256:(core + 1) * 256],
+                    in_=wgrp[:, g, core * 1024:(core + 1) * 1024])
+
+        def weights_core2(wts, dst2):
+            for g in range(2):
+                for k in range(2, 4):
+                    src = wts[k][:].rearrange("p (b a g u c) -> p c g b a u", b=4, c=2, a=16, g=2)
+                    nc.scalar.copy(
+                        out=dst2[:, g, :, 4 * k:4 * k + 4], in_=src[:, 1, g].rearrange("p b a u -> p a b u"))
+            quantise_core(1)
 
         grouped_of = {}
         bank_of = {}
@@ -173,31 +185,43 @@ def tile_linear_pa_kernel(tc, x, w0, core1, core2, out):
             p2 = stage.tile([P, CH, 256], F32, tag="p2")
             p2_of[c] = p2
             for h in range(2):
-                nc.vector.tensor_tensor(
-                    out=p2[:, 2 * h:2 * h + 2, :].rearrange("p t (q r) -> p t q r", q=16),
-                    in0=bank_of[(c, 1, h)][:].rearrange("p (t q r) -> p t q r", t=2, q=16),
-                    in1=w1_of[c][:, h * 32:(h + 1) * 32].rearrange(
-                        "p (t q) -> p t q", t=2).unsqueeze(3).to_broadcast([P, 2, 16, 16]),
-                    op=MULT,
-                )
+                w1_h = w1_of[c][:, h * 32:(h + 1) * 32].rearrange("p (t q) -> p t q", t=2)
+                if c == NCH - 1:
+                    nc.vector.tensor_tensor(
+                        out=p2[:, 2 * h:2 * h + 2, :].rearrange("p t (r q) -> p t r q", q=16),
+                        in0=bank_of[(c, 1, h)][:].rearrange("p (t q r) -> p t r q", t=2, q=16),
+                        in1=w1_h.unsqueeze(2).to_broadcast([P, 2, 16, 16]),
+                        op=MULT,
+                    )
+                else:
+                    nc.vector.tensor_tensor(
+                        out=p2[:, 2 * h:2 * h + 2, :].rearrange("p t (q r) -> p t q r", q=16),
+                        in0=bank_of[(c, 1, h)][:].rearrange("p (t q r) -> p t q r", t=2, q=16),
+                        in1=w1_h.unsqueeze(3).to_broadcast([P, 2, 16, 16]),
+                        op=MULT,
+                    )
 
         def sum_b(c):
             p2 = p2_of[c]
             o_view = out_sb[:, c * CH * R:(c + 1) * CH * R].rearrange("p (t r) -> p t r", r=R)
-            eng = nc.vector if c == NCH - 1 else nc.gpsimd
-            for half in (128, 64, 32):
-                eng.tensor_tensor(
-                    out=p2[:, :, 0:half], in0=p2[:, :, 0:half], in1=p2[:, :, half:2 * half], op=ADD)
-            eng.tensor_tensor(out=o_view, in0=p2[:, :, 0:16], in1=p2[:, :, 16:32], op=ADD)
+            if c == NCH - 1:
+                nc.vector.tensor_reduce(
+                    out=o_view, in_=p2[:].rearrange("p t (r q) -> p t r q", q=16), axis=AXIS_X, op=ADD)
+            else:
+                for half in (128, 64, 32):
+                    nc.gpsimd.tensor_tensor(
+                        out=p2[:, :, 0:half], in0=p2[:, :, 0:half], in1=p2[:, :, half:2 * half], op=ADD)
+                nc.gpsimd.tensor_tensor(out=o_view, in0=p2[:, :, 0:16], in1=p2[:, :, 16:32], op=ADD)
             nc.sync.dma_start(out=outv[:, c * CH:(c + 1) * CH, :], in_=o_view)
 
         def live(c):
             return 0 <= c < NCH
 
         whole = (0, 1, 2, 3)
-        weights()
+        wts_left, dst2_left = weights()
         transposes(0, whole, on_vector=(3,))
         quantise(0, parts=2)
+        weights_core2(wts_left, dst2_left)
         transposes(1, (0, 1))
         passes(0, 0)
         transposes(1, (2, 3))

@@ -54,8 +54,14 @@ def tile_linear_pa_kernel(tc, x, w0, core1, core2, out):
         for c in range(NCH):
             nc.sync.dma_start(out=xs[c][:], in_=xv[:, c * CH:(c + 1) * CH, :])
 
+        zeros = keep.tile([P, P], F32)
+        nc.vector.memset(zeros[:], 0.0)
         ident = keep.tile([P, P], F32)
         make_identity(nc, ident[:])
+
+        def idle_matmuls(bank_columns, count):
+            for i in range(count):
+                nc.tensor.matmul(out=bank_columns, lhsT=zeros[:], rhs=zeros[:], start=True, stop=True)
         out_sb = keep.tile([P, TILES * R], F32)
 
         wgrp = keep.tile([P, 2, 2048], BF16, align_bytes=64)
@@ -79,6 +85,8 @@ def tile_linear_pa_kernel(tc, x, w0, core1, core2, out):
                 pool = ps_a if k < 2 else ps_b
                 wt = pool.tile([P, 512], F32, tag="bank%d" % (k // 2))
                 wts.append(wt)
+                if k == 0:
+                    idle_matmuls(wt[:, 0:P], 16)
                 for bb in range(4):
                     b = 4 * k + bb
                     nc.tensor.transpose(
@@ -119,7 +127,7 @@ def tile_linear_pa_kernel(tc, x, w0, core1, core2, out):
         p2_of = {}
         w1_of = {}
 
-        def transposes(c, tiles, on_vector=()):
+        def transposes(c, tiles, on_vector=(), idle_first=0):
             if c not in grouped_of:
                 new_grouped = stage.tile([P, CH * 1024], BF16, align_bytes=64, tag="grouped")
                 grouped_of[c] = new_grouped
@@ -127,6 +135,8 @@ def tile_linear_pa_kernel(tc, x, w0, core1, core2, out):
             for jj in tiles:
                 xt = ps_t.tile([P, 512], F32, tag="xt")
                 xw = xs[c][:, jj, :].bitcast(F32)
+                if jj == tiles[0]:
+                    idle_matmuls(xt[:, 0:P], idle_first)
                 for k in range(4):
                     nc.tensor.transpose(xt[:, k * P:(k + 1) * P], xw[:, k * P:(k + 1) * P], ident[:])
                 dst = grouped[:, jj * 1024:(jj + 1) * 1024].bitcast(F32).rearrange(
@@ -219,10 +229,10 @@ def tile_linear_pa_kernel(tc, x, w0, core1, core2, out):
 
         whole = (0, 1, 2, 3)
         wts_left, dst2_left = weights()
-        transposes(0, whole, on_vector=(3,))
+        transposes(0, whole, on_vector=(3,), idle_first=2)
         quantise(0, parts=2)
         weights_core2(wts_left, dst2_left)
-        transposes(1, (0, 1))
+        transposes(1, (0, 1), idle_first=2)
         passes(0, 0)
         transposes(1, (2, 3))
         transposes(2, whole)

@@ -236,6 +236,7 @@ def tile_linear_pa_kernel(tc, x, w0, core1, core2, out):
         passes(0, 0)
         transposes(1, (2, 3))
         transposes(2, whole)
+        transposes(3, whole)
         mult_a(0)
         sum_a(0)
         quantise(1)
@@ -246,8 +247,8 @@ def tile_linear_pa_kernel(tc, x, w0, core1, core2, out):
             passes(c, 1)
             if c > 0:
                 sum_a(c)
-            if live(c + 3):
-                transposes(c + 3, whole)
+            if live(c + 4):
+                transposes(c + 4, whole)
             if live(c + 1):
                 mult_a(c + 1)
             if live(c + 2):

from contextlib import ExitStack

import concourse.mybir as mybir
from concourse.masks import make_identity

F32 = mybir.dt.float32
BF16 = mybir.dt.bfloat16
U32 = mybir.dt.uint32
U8 = mybir.dt.uint8
FP8X4 = mybir.dt.float8_e4m3fn_x4
ADD = mybir.AluOpType.add
MULT = mybir.AluOpType.mult
AXIS_X = mybir.AxisListType.X

P = 128
TOKENS = 4096
D = 1024
R = 16
TILES = TOKENS // P
CH = 4
NCH = TILES // CH
FLOPS = 2 * TOKENS * D * 512 + 4 * TOKENS * 256


def tile_linear_pa_kernel(tc, x, w0, core1, core2, out):
    nc = tc.nc
    xv = x.flatten_outer_dims().rearrange("(p j) d -> p j d", j=TILES)
    w0v = w0.flatten_outer_dims().rearrange("(p j) r -> p (j r)", j=TILES)
    outv = out.flatten_outer_dims().rearrange("(p j) r -> p j r", j=TILES)

    with ExitStack() as ctx:
        keep = ctx.enter_context(tc.tile_pool(name="keep", bufs=1))
        stage = ctx.enter_context(tc.tile_pool(name="stage", bufs=3))
        ps_t = ctx.enter_context(tc.psum_pool(name="ps_t", bufs=4))
        ps_a = ctx.enter_context(tc.psum_pool(name="ps_a", bufs=2))
        ps_b = ctx.enter_context(tc.psum_pool(name="ps_b", bufs=2))
        ctx.enter_context(tc.manual_schedule())

        wl = keep.tile([P, 4096], BF16)
        xs = []
        xcodes = []
        xscales = []
        for c in range(NCH):
            x_sb = keep.tile([P, CH, D], BF16, name="x_sb%d" % c)
            xs.append(x_sb)
            codes = keep.tile([P, CH * 256], U32, align_bytes=64, name="codes%d" % c)
            xcodes.append(codes)
            scales = keep.tile([P, CH * 256], U8, align_bytes=64, name="scales%d" % c)
            xscales.append(scales)
        nc.sync.dma_start(out=wl[0:128:2, :], in_=core1.rearrange("a (c l) b -> (a c) (l b)", c=4))
        nc.scalar.dma_start(out=wl[1:128:2, :], in_=core2.rearrange("a (c l) b -> (a c) (l b)", c=4))
        w0_sb = keep.tile([P, TILES * R], BF16)
        nc.scalar.dma_start(out=w0_sb[:], in_=w0v)
        for c in range(NCH):
            nc.sync.dma_start(out=xs[c][:], in_=xv[:, c * CH:(c + 1) * CH, :])

        zeros = keep.tile([P, P], F32)
        nc.vector.memset(zeros[:], 0.0)
        ident = keep.tile([P, P], F32)
        make_identity(nc, ident[:])

        def idle_matmuls(bank_columns, count):
            for i in range(count):
                nc.tensor.matmul(out=bank_columns, lhsT=zeros[:], rhs=zeros[:], start=True, stop=True)
        out_sb = keep.tile([P, TILES * R], F32)

        wgrp = keep.tile([P, 2, 2048], BF16, align_bytes=64)
        wcodes = keep.tile([P, 2, 512], U32, align_bytes=64)
        wscales = keep.tile([P, 2, 512], U8, align_bytes=64)
        wd = keep.tile([P, 4096], BF16)

        def weights():
            wl_v = wl[:].rearrange("p (l b) -> p l b", b=16)
            for k, eng in ((0, "v"), (2, "s"), (3, "g"), (1, "v")):
                dst = wd[:, k * 1024:(k + 1) * 1024].rearrange("p (b l) -> p l b", b=4)
                src = wl_v[:, :, 4 * k:4 * k + 4]
                if eng == "v":
                    nc.vector.tensor_copy(out=dst, in_=src)
                elif eng == "s":
                    nc.scalar.copy(out=dst, in_=src)
                else:
                    nc.gpsimd.tensor_scalar(out=dst, in0=src, scalar1=1.0, scalar2=0.0, op0=MULT, op1=ADD)
            wts = []
            for k in range(4):
                pool = ps_a if k < 2 else ps_b
                wt = pool.tile([P, 512], F32, tag="bank%d" % (k // 2))
                wts.append(wt)
                if k == 0:
                    idle_matmuls(wt[:, 0:P], 16)
                for bb in range(4):
                    b = 4 * k + bb
                    nc.tensor.transpose(
                        wt[:, bb * P:(bb + 1) * P], wd[:, b * 256:(b + 1) * 256].bitcast(F32), ident[:])
            words = wgrp[:].rearrange("p g n -> p (g n)").bitcast(F32)
            dst1 = words.rearrange("p (g c b a u) -> p c g b a u", g=2, c=2, b=16, a=16)[:, 0]
            dst2 = words.rearrange("p (g c a b u) -> p c g a b u", g=2, c=2, b=16, a=16)[:, 1]
            for k in range(2):
                src = wts[k][:].rearrange("p (b a g u c) -> p c g b a u", b=4, c=2, a=16, g=2)
                nc.vector.tensor_copy(out=dst1[:, :, 4 * k:4 * k + 4], in_=src[:, 0])
                nc.vector.tensor_copy(
                    out=dst2[:, :, :, 4 * k:4 * k + 4], in_=src[:, 1].rearrange("p g b a u -> p g a b u"))
            for g in range(2):
                for k in range(2, 4):
                    src = wts[k][:].rearrange("p (b a g u c) -> p c g b a u", b=4, c=2, a=16, g=2)
                    nc.scalar.copy(out=dst1[:, g, 4 * k:4 * k + 4], in_=src[:, 0, g])
            quantise_core(0)
            return wts, dst2

        def quantise_core(core):
            for g in range(2):
                nc.vector.quantize_mx(
                    out=wcodes[:, g, core * 256:(core + 1) * 256].bitcast(FP8X4),
                    scales=wscales[:, g, core * 256:(core + 1) * 256],
                    in_=wgrp[:, g, core * 1024:(core + 1) * 1024])

        def weights_core2(wts, dst2):
            for g in range(2):
                for k in range(2, 4):
                    src = wts[k][:].rearrange("p (b a g u c) -> p c g b a u", b=4, c=2, a=16, g=2)
                    nc.scalar.copy(
                        out=dst2[:, g, :, 4 * k:4 * k + 4], in_=src[:, 1, g].rearrange("p b a u -> p a b u"))
            quantise_core(1)

        grouped_of = {}
        bank_of = {}
        p1_of = {}
        p2_of = {}
        w1_of = {}

        def transposes(c, tiles, on_vector=(), idle_first=0):
            if c not in grouped_of:
                new_grouped = stage.tile([P, CH * 1024], BF16, align_bytes=64, tag="grouped")
                grouped_of[c] = new_grouped
            grouped = grouped_of[c]
            for jj in tiles:
                xt = ps_t.tile([P, 512], F32, tag="xt")
                xw = xs[c][:, jj, :].bitcast(F32)
                if jj == tiles[0]:
                    idle_matmuls(xt[:, 0:P], idle_first)
                for k in range(4):
                    nc.tensor.transpose(xt[:, k * P:(k + 1) * P], xw[:, k * P:(k + 1) * P], ident[:])
                dst = grouped[:, jj * 1024:(jj + 1) * 1024].bitcast(F32).rearrange(
                    "p (g r u) -> p g r u", g=2, u=2)
                src = xt[:].rearrange("p (g u r) -> p g r u", g=2, u=2)
                if jj in on_vector:
                    nc.vector.tensor_copy(out=dst, in_=src)
                else:
                    nc.scalar.copy(out=dst, in_=src)

        def quantise(c, parts=1):
            w = CH * 256 // parts
            for h in range(parts):
                nc.vector.quantize_mx(
                    out=xcodes[c][:, h * w:(h + 1) * w].bitcast(FP8X4),
                    scales=xscales[c][:, h * w:(h + 1) * w],
                    in_=grouped_of[c][:, 4 * h * w:4 * (h + 1) * w])

        def passes(c, core):
            pool = ps_a if core == 0 else ps_b
            for h in range(2):
                bank = pool.tile([P, 512], F32, tag="bank%d" % core)
                bank_of[(c, core, h)] = bank
                for t in range(2):
                    jj = 2 * h + t
                    for g in range(2):
                        cols = slice((jj * 2 + g) * P, (jj * 2 + g + 1) * P)
                        nc.tensor.matmul_mx(
                            out=bank[:, t * 256:(t + 1) * 256],
                            lhsT=xcodes[c][:, cols].bitcast(FP8X4), lhsT_scale=xscales[c][:, cols],
                            rhs=wcodes[:, g, core * 256:(core + 1) * 256].bitcast(FP8X4),
                            rhs_scale=wscales[:, g, core * 256:(core + 1) * 256],
                            start=(g == 0), stop=(g == 1),
                        )

        def mult_a(c):
            p1 = stage.tile([P, CH * 256], F32, tag="p1")
            p1_of[c] = p1
            for h in range(2):
                j0 = c * CH + 2 * h
                nc.vector.tensor_tensor(
                    out=p1[:, h * 512:(h + 1) * 512].rearrange("p (t q r) -> p t q r", t=2, q=16),
                    in0=bank_of[(c, 0, h)][:].rearrange("p (t q r) -> p t q r", t=2, q=16),
                    in1=w0_sb[:, j0 * R:(j0 + 2) * R].rearrange(
                        "p (t r) -> p t r", t=2).unsqueeze(2).to_broadcast([P, 2, 16, 16]),
                    op=MULT,
                )

        def sum_a(c):
            w1 = stage.tile([P, CH * 16], F32, tag="w1")
            w1_of[c] = w1
            nc.vector.tensor_reduce(
                out=w1[:], in_=p1_of[c][:].rearrange("p (n r) -> p n r", r=16), axis=AXIS_X, op=ADD)

        def mult_b(c):
            p2 = stage.tile([P, CH, 256], F32, tag="p2")
            p2_of[c] = p2
            for h in range(2):
                w1_h = w1_of[c][:, h * 32:(h + 1) * 32].rearrange("p (t q) -> p t q", t=2)
                if c == NCH - 1:
                    nc.vector.tensor_tensor(
                        out=p2[:, 2 * h:2 * h + 2, :].rearrange("p t (r q) -> p t r q", q=16),
                        in0=bank_of[(c, 1, h)][:].rearrange("p (t q r) -> p t r q", t=2, q=16),
                        in1=w1_h.unsqueeze(2).to_broadcast([P, 2, 16, 16]),
                        op=MULT,
                    )
                else:
                    nc.vector.tensor_tensor(
                        out=p2[:, 2 * h:2 * h + 2, :].rearrange("p t (q r) -> p t q r", q=16),
                        in0=bank_of[(c, 1, h)][:].rearrange("p (t q r) -> p t q r", t=2, q=16),
                        in1=w1_h.unsqueeze(3).to_broadcast([P, 2, 16, 16]),
                        op=MULT,
                    )

        def sum_b(c):
            p2 = p2_of[c]
            o_view = out_sb[:, c * CH * R:(c + 1) * CH * R].rearrange("p (t r) -> p t r", r=R)
            if c == NCH - 1:
                nc.vector.tensor_reduce(
                    out=o_view, in_=p2[:].rearrange("p t (r q) -> p t r q", q=16), axis=AXIS_X, op=ADD)
            else:
                for half in (128, 64, 32):
                    nc.gpsimd.tensor_tensor(
                        out=p2[:, :, 0:half], in0=p2[:, :, 0:half], in1=p2[:, :, half:2 * half], op=ADD)
                nc.gpsimd.tensor_tensor(out=o_view, in0=p2[:, :, 0:16], in1=p2[:, :, 16:32], op=ADD)
            nc.sync.dma_start(out=outv[:, c * CH:(c + 1) * CH, :], in_=o_view)

        def live(c):
            return 0 <= c < NCH

        whole = (0, 1, 2, 3)
        wts_left, dst2_left = weights()
        transposes(0, whole, on_vector=(3,), idle_first=2)
        quantise(0, parts=2)
        weights_core2(wts_left, dst2_left)
        transposes(1, (0, 1), idle_first=2)
        passes(0, 0)
        transposes(1, (2, 3))
        transposes(2, whole)
        transposes(3, whole)
        mult_a(0)
        sum_a(0)
        quantise(1)
        passes(1, 0)
        for c in range(NCH):
            if live(c + 2):
                quantise(c + 2)
            passes(c, 1)
            if c > 0:
                sum_a(c)
            if live(c + 4):
                transposes(c + 4, whole)
            if live(c + 1):
                mult_a(c + 1)
            if live(c + 2):
                passes(c + 2, 0)
            mult_b(c)
            sum_b(c)
